import numpy as np
import ml_dtypes


def mxq(x, axis, fmt="e4m3"):
    dtype, down = {"e4m3": (ml_dtypes.float8_e4m3fn, 7), "e5m2": (ml_dtypes.float8_e5m2, 14)}[fmt]
    v = np.moveaxis(np.asarray(x, np.float32).astype(ml_dtypes.bfloat16).astype(np.float64), axis, -1)
    blocks = v.reshape(v.shape[:-1] + (-1, 32))
    amax = np.abs(blocks).max(-1, keepdims=True)
    byte = np.maximum(np.where(amax > 0, np.frexp(amax)[1] - 1 + 127, 0) - down, 1)
    scale = np.exp2(byte - 127.0)
    codes = (blocks / scale).astype(np.float32).astype(dtype).astype(np.float64)
    return np.moveaxis((codes * scale).reshape(v.shape), -1, axis)


WIDE = False


def mx_kscale(k):
    if not WIDE:
        return np.ones(k)
    levels = np.array([10, -10, 5, -5, 0])
    a = np.random.permutation(np.resize(levels, k // 512 * 4)).reshape(k // 512, 4)
    idx = np.arange(k)
    return np.exp2(a[idx // 512, idx % 128 // 32])


BF16 = ml_dtypes.bfloat16


def bf(x):
    return np.asarray(x, np.float32).astype(BF16)


def f64(x):
    return np.asarray(x).astype(np.float64)


B, N, AB, MAXN, BB, H = 2, 64, 704, 511, 64, 512
TAIL = AB - (MAXN + 1)
AF = AB + TAIL
FB = AF + BB + BB


def setup_inputs():
    s = mx_kscale(FB)
    sa, sb = s[:AB], s[AF:AF + BB]
    se = np.concatenate([sa, sa[MAXN + 1:], sb, sb])
    return {"f_atoms": bf(np.random.standard_normal((B, N, AB)) * sa),
            "f_bonds": bf(np.random.standard_normal((B, N, N, BB)) * sb),
            "adj": bf(np.random.uniform(size=(B, N, N)) * 4.0 / N),
            "W_i_w": bf(np.random.standard_normal((H, FB)) * 0.1 * N / np.sqrt(FB) / se)}


def reference(f_atoms, f_bonds, adj, W_i_w):
    f_atoms, f_bonds, adj = f64(f_atoms), f64(f_bonds), f64(adj)
    fa = np.concatenate([f_atoms, f_atoms[:, :, MAXN + 1:]], axis=-1)
    fa_exp = np.broadcast_to(fa[:, :, None, :], (B, N, N, AF))
    fb = np.concatenate([fa_exp, f_bonds, f_bonds], axis=-1)
    return mxq(adj[..., None] * fb, 3, "e4m3") @ mxq(f64(W_i_w).T, 0, "e4m3")

@@ -1,0 +1,196 @@
+from contextlib import ExitStack
+
+import concourse.mybir as mybir
+from concourse.masks import make_identity
+
+F32 = mybir.dt.float32
+BF16 = mybir.dt.bfloat16
+U32 = mybir.dt.uint32
+U8 = mybir.dt.uint8
+FP8X4 = mybir.dt.float8_e4m3fn_x4
+MULT = mybir.AluOpType.mult
+
+P = 128
+N = 64
+AB = 704
+BB = 64
+H = 512
+G = 4
+NG = N // G
+NS = 2 * G
+FLOPS = 2 * 2 * N * N * 1024 * H
+
+W_BLOCKS = ((0, 0, 512), (512, 896, 64), (576, 512, 192), (768, 960, 64), (832, 704, 192))
+
+
+def tile_mpnencoder_pa_t_kernel(tc, f_atoms, f_bonds, adj, W_i_w, out):
+    nc = tc.nc
+    with ExitStack() as ctx:
+        keep = ctx.enter_context(tc.tile_pool(name="keep", bufs=1))
+        st_in = ctx.enter_context(tc.tile_pool(name="st_in", bufs=4))
+        st_cd = ctx.enter_context(tc.tile_pool(name="st_cd", bufs=3))
+        st_out = ctx.enter_context(tc.tile_pool(name="st_out", bufs=3))
+        ps_o = ctx.enter_context(tc.psum_pool(name="ps_o", bufs=4))
+        ps_j = ctx.enter_context(tc.psum_pool(name="ps_j", bufs=2))
+        ps_t = ctx.enter_context(tc.psum_pool(name="ps_t", bufs=2))
+        ctx.enter_context(tc.manual_schedule())
+
+        ident = keep.tile([P, P], F32, name="ident")
+        adj_sb = keep.tile([P, N], BF16, name="adj_sb")
+        adj2 = keep.tile([P, N, 2], BF16, name="adj2")
+        fa_sb = keep.tile([P, AB], BF16, name="fa_sb")
+        fa_t0 = keep.tile([P, 512], BF16, name="fa_t0")
+        f1 = keep.tile([P, NS, P], F32, name="f1")
+        b_sb = keep.tile([P, N * BB + 192], BF16, name="b_sb")
+        w_sb = keep.tile([P, 4, 1024], BF16, name="w_sb")
+        w_in = keep.tile([P, 2, 2048], BF16, name="w_in", align_bytes=64)
+        w_cd = keep.tile([P, 2, H], U32, name="w_cd", align_bytes=64)
+        w_sc = keep.tile([P, 2, H], U8, name="w_sc", align_bytes=64)
+
+        nc.sync.dma_start(out=adj_sb[:], in_=adj.rearrange("b m n -> (b m) n"))
+        nc.sync.dma_start(out=fa_sb[:], in_=f_atoms.rearrange("b m f -> (b m) f"))
+        bonds_v = f_bonds.rearrange("b m n f -> (b m) (n f)")
+        nc.sync.dma_start(out=b_sb[:, 0:1024], in_=bonds_v[:, 0:1024])
+        w_v = W_i_w.rearrange("(t p) f -> p t f", p=P)
+        for dst, src, width in W_BLOCKS:
+            nc.sync.dma_start(out=w_sb[:, :, dst:dst + width], in_=w_v[:, :, src:src + width])
+        for c in range(1, 4):
+            nc.sync.dma_start(out=b_sb[:, 1024 * c:1024 * (c + 1)], in_=bonds_v[:, 1024 * c:1024 * (c + 1)])
+        out_v = out.rearrange("b m n h -> (b m) n h")
+
+        make_identity(nc, ident[:])
+        nc.vector.memset(b_sb[:, N * BB:N * BB + 192], 0.0)
+        nc.vector.tensor_copy(out=adj2[:], in_=adj_sb[:].unsqueeze(2).to_broadcast([P, N, 2]))
+
+        adj2_w = adj2[:].rearrange("p n e -> p (n e)").bitcast(F32)
+        fa_w = fa_sb[:].bitcast(F32)
+        b_w = b_sb[:].bitcast(F32)
+        w_w = w_sb[:].bitcast(F32)
+
+        ft = ps_t.tile([P, 3, P], F32, tag="T", name="ft")
+        for k, first in enumerate((0, 128, 224)):
+            nc.tensor.transpose(ft[:, k, :], fa_w[:, first:first + P], ident[:])
+        nc.vector.tensor_copy(
+            out=fa_t0[:].bitcast(F32).rearrange("p (w u) -> p w u", u=2),
+            in_=ft[:, 0:2, :].rearrange("p u w -> p w u"),
+        )
+        nc.scalar.copy(out=f1[:], in_=ft[:, 2:3, :].to_broadcast([P, NS, P]))
+
+        def twice(words):
+            return (
+                words.bitcast(BF16)
+                .rearrange("p n (w e) -> p n w e", e=2)
+                .unsqueeze(3)
+                .to_broadcast([P, G, P, 2, 2])
+            )
+
+        j_of = {}
+        t_of = {}
+        in_of = {}
+        cd_of = {}
+
+        def flips(g):
+            j_ps = ps_j.tile([P, G, P], F32, tag="J", name="j_ps")
+            t_ps = ps_t.tile([P, G, P], F32, tag="T", name="t_ps")
+            for i in range(G):
+                n = G * g + i
+                nc.tensor.transpose(j_ps[:, i, :], adj2_w[:, n:n + 1].to_broadcast([P, P]), ident[:])
+            for i in range(G):
+                n = G * g + i
+                nc.tensor.transpose(t_ps[:, i, :], b_w[:, 32 * n:32 * n + P], ident[:])
+            j_of[g] = j_ps
+            t_of[g] = t_ps
+
+        def slot(g):
+            return G * (g % 2)
+
+        def bonds(g):
+            nc.scalar.copy(out=f1[0:32, slot(g):slot(g) + G, :], in_=t_of[g][0:32, :, :])
+
+        def gate0(g):
+            g_in = st_in.tile([P, 2, G * 512], BF16, tag="IN", name="g_in", align_bytes=64)
+            in_of[g] = g_in
+            nc.vector.tensor_tensor(
+                out=g_in[:, 0, :].rearrange("p (n w u e) -> p n w u e", n=G, w=P, u=2),
+                in0=fa_t0[:].rearrange("p (w u e) -> p w u e", u=2, e=2).unsqueeze(1).to_broadcast([P, G, P, 2, 2]),
+                in1=twice(j_of[g][:]),
+                op=MULT,
+            )
+
+        def gate1(g):
+            nc.vector.tensor_tensor(
+                out=in_of[g][:, 1, :].rearrange("p (n w u e) -> p n w u e", n=G, w=P, u=2),
+                in0=twice(f1[:, slot(g):slot(g) + G, :]),
+                in1=twice(j_of[g][:]),
+                op=MULT,
+            )
+
+        def quant(g):
+            cd = st_cd.tile([P, 2, G * P], U32, tag="CD", name="cd", align_bytes=64)
+            sc = st_cd.tile([P, 2, G * P], U8, tag="SC", name="sc", align_bytes=64)
+            cd_of[g] = (cd, sc)
+            nc.vector.quantize_mx(
+                out=cd[:].rearrange("p c w -> p (c w)").bitcast(FP8X4),
+                scales=sc[:].rearrange("p c w -> p (c w)"),
+                in_=in_of[g][:].rearrange("p c w -> p (c w)"),
+            )
+
+        def project(g):
+            cd, sc = cd_of[g]
+            o_sb = st_out.tile([P, G, H], F32, tag="OS", name="o_sb")
+            for i in range(G):
+                o_ps = ps_o.tile([P, H], F32, tag="O", name="o_ps")
+                for c in range(2):
+                    nc.tensor.matmul_mx(
+                        out=o_ps[:],
+                        lhsT=cd[:, c, P * i:P * (i + 1)].bitcast(FP8X4),
+                        lhsT_scale=sc[:, c, P * i:P * (i + 1)],
+                        rhs=w_cd[:, c, :].bitcast(FP8X4),
+                        rhs_scale=w_sc[:, c, :],
+                        start=(c == 0),
+                        stop=(c == 1),
+                    )
+                nc.scalar.copy(out=o_sb[:, i, :], in_=o_ps[:])
+            nc.sync.dma_start(out=out_v[:, G * g:G * (g + 1), :], in_=o_sb[:])
+
+        flips(0)
+        bonds(0)
+        flips(1)
+        bonds(1)
+        gate0(0)
+        gate1(0)
+        gate0(1)
+        gate1(1)
+
+        for c in range(2):
+            for half in range(2):
+                wt = ps_o.tile([P, 2, 256], F32, tag="O", name="wt")
+                for u in range(2):
+                    for t2 in range(2):
+                        nc.tensor.transpose(
+                            wt[:, u, P * t2:P * (t2 + 1)],
+                            w_w[:, 2 * half + t2, 256 * c + P * u:256 * c + P * (u + 1)],
+                            ident[:],
+                        )
+                dst = w_in[:, c, :].bitcast(F32).rearrange("p (h u) -> p h u", u=2)[:, 256 * half:256 * (half + 1), :]
+                src = wt[:].rearrange("p u h -> p h u")
+                if half == 0:
+                    nc.vector.tensor_copy(out=dst, in_=src)
+                else:
+                    nc.scalar.copy(out=dst, in_=src)
+        for c in range(2):
+            nc.vector.quantize_mx(out=w_cd[:, c, :].bitcast(FP8X4), scales=w_sc[:, c, :], in_=w_in[:, c, :])
+
+        flips(2)
+        bonds(2)
+        for g in range(NG):
+            if g + 2 < NG:
+                gate0(g + 2)
+            quant(g)
+            if g + 2 < NG:
+                gate1(g + 2)
+            if g + 3 < NG:
+                flips(g + 3)
+            project(g)
+            if g + 3 < NG:
+                bonds(g + 3)

@@ -16,7 +16,8 @@ AB = 704
 BB = 64
 H = 512
 G = 4
-NG = N // G
+SIZES = (4,) * 15 + (2, 1, 1)
+NG = len(SIZES)
 NS = 2 * G
 FLOPS = 2 * 2 * N * N * 1024 * H
 
@@ -25,6 +26,7 @@ W_BLOCKS = ((0, 0, 512), (512, 896, 64), (576, 512, 192), (768, 960, 64), (832, 
 
 def tile_mpnencoder_pa_t_kernel(tc, f_atoms, f_bonds, adj, W_i_w, out):
     nc = tc.nc
+    FIRST = [sum(SIZES[:g]) for g in range(NG)]
     with ExitStack() as ctx:
         keep = ctx.enter_context(tc.tile_pool(name="keep", bufs=1))
         st_in = ctx.enter_context(tc.tile_pool(name="st_in", bufs=4))
@@ -76,12 +78,12 @@ def tile_mpnencoder_pa_t_kernel(tc, f_atoms, f_bonds, adj, W_i_w, out):
         )
         nc.scalar.copy(out=f1[:], in_=ft[:, 2:3, :].to_broadcast([P, NS, P]))
 
-        def twice(words):
+        def twice(words, s):
             return (
                 words.bitcast(BF16)
                 .rearrange("p n (w e) -> p n w e", e=2)
                 .unsqueeze(3)
-                .to_broadcast([P, G, P, 2, 2])
+                .to_broadcast([P, s, P, 2, 2])
             )
 
         j_of = {}
@@ -92,11 +94,11 @@ def tile_mpnencoder_pa_t_kernel(tc, f_atoms, f_bonds, adj, W_i_w, out):
         def flips(g):
             j_ps = ps_j.tile([P, G, P], F32, tag="J", name="j_ps")
             t_ps = ps_t.tile([P, G, P], F32, tag="T", name="t_ps")
-            for i in range(G):
-                n = G * g + i
+            for i in range(SIZES[g]):
+                n = FIRST[g] + i
                 nc.tensor.transpose(j_ps[:, i, :], adj2_w[:, n:n + 1].to_broadcast([P, P]), ident[:])
-            for i in range(G):
-                n = G * g + i
+            for i in range(SIZES[g]):
+                n = FIRST[g] + i
                 nc.tensor.transpose(t_ps[:, i, :], b_w[:, 32 * n:32 * n + P], ident[:])
             j_of[g] = j_ps
             t_of[g] = t_ps
@@ -105,53 +107,58 @@ def tile_mpnencoder_pa_t_kernel(tc, f_atoms, f_bonds, adj, W_i_w, out):
             return G * (g % 2)
 
         def bonds(g):
-            nc.scalar.copy(out=f1[0:32, slot(g):slot(g) + G, :], in_=t_of[g][0:32, :, :])
+            s = SIZES[g]
+            nc.scalar.copy(out=f1[0:32, slot(g):slot(g) + s, :], in_=t_of[g][0:32, 0:s, :])
 
         def gate0(g):
-            g_in = st_in.tile([P, 2, G * 512], BF16, tag="IN", name="g_in", align_bytes=64)
+            s = SIZES[g]
+            g_in = st_in.tile([P, G, 2, 512], BF16, tag="IN", name="g_in", align_bytes=64)
             in_of[g] = g_in
             nc.vector.tensor_tensor(
-                out=g_in[:, 0, :].rearrange("p (n w u e) -> p n w u e", n=G, w=P, u=2),
-                in0=fa_t0[:].rearrange("p (w u e) -> p w u e", u=2, e=2).unsqueeze(1).to_broadcast([P, G, P, 2, 2]),
-                in1=twice(j_of[g][:]),
+                out=g_in[:, 0:s, 0, :].rearrange("p n (w u e) -> p n w u e", u=2, e=2),
+                in0=fa_t0[:].rearrange("p (w u e) -> p w u e", u=2, e=2).unsqueeze(1).to_broadcast([P, s, P, 2, 2]),
+                in1=twice(j_of[g][:, 0:s, :], s),
                 op=MULT,
             )
 
         def gate1(g):
+            s = SIZES[g]
             nc.vector.tensor_tensor(
-                out=in_of[g][:, 1, :].rearrange("p (n w u e) -> p n w u e", n=G, w=P, u=2),
-                in0=twice(f1[:, slot(g):slot(g) + G, :]),
-                in1=twice(j_of[g][:]),
+                out=in_of[g][:, 0:s, 1, :].rearrange("p n (w u e) -> p n w u e", u=2, e=2),
+                in0=twice(f1[:, slot(g):slot(g) + s, :], s),
+                in1=twice(j_of[g][:, 0:s, :], s),
                 op=MULT,
             )
 
         def quant(g):
-            cd = st_cd.tile([P, 2, G * P], U32, tag="CD", name="cd", align_bytes=64)
-            sc = st_cd.tile([P, 2, G * P], U8, tag="SC", name="sc", align_bytes=64)
+            s = SIZES[g]
+            cd = st_cd.tile([P, G, 2, P], U32, tag="CD", name="cd", align_bytes=64)
+            sc = st_cd.tile([P, G, 2, P], U8, tag="SC", name="sc", align_bytes=64)
             cd_of[g] = (cd, sc)
             nc.vector.quantize_mx(
-                out=cd[:].rearrange("p c w -> p (c w)").bitcast(FP8X4),
-                scales=sc[:].rearrange("p c w -> p (c w)"),
-                in_=in_of[g][:].rearrange("p c w -> p (c w)"),
+                out=cd[:, 0:s].rearrange("p n c w -> p (n c w)").bitcast(FP8X4),
+                scales=sc[:, 0:s].rearrange("p n c w -> p (n c w)"),
+                in_=in_of[g][:, 0:s].rearrange("p n c k -> p (n c k)"),
             )
 
         def project(g):
             cd, sc = cd_of[g]
             o_sb = st_out.tile([P, G, H], F32, tag="OS", name="o_sb")
-            for i in range(G):
+            s = SIZES[g]
+            for i in range(s):
                 o_ps = ps_o.tile([P, H], F32, tag="O", name="o_ps")
                 for c in range(2):
                     nc.tensor.matmul_mx(
                         out=o_ps[:],
-                        lhsT=cd[:, c, P * i:P * (i + 1)].bitcast(FP8X4),
-                        lhsT_scale=sc[:, c, P * i:P * (i + 1)],
+                        lhsT=cd[:, i, c, :].bitcast(FP8X4),
+                        lhsT_scale=sc[:, i, c, :],
                         rhs=w_cd[:, c, :].bitcast(FP8X4),
                         rhs_scale=w_sc[:, c, :],
                         start=(c == 0),
                         stop=(c == 1),
                     )
                 nc.scalar.copy(out=o_sb[:, i, :], in_=o_ps[:])
-            nc.sync.dma_start(out=out_v[:, G * g:G * (g + 1), :], in_=o_sb[:])
+            nc.sync.dma_start(out=out_v[:, FIRST[g]:FIRST[g] + s, :], in_=o_sb[:, 0:s, :])
 
         flips(0)
         bonds(0)
@@ -174,10 +181,7 @@ def tile_mpnencoder_pa_t_kernel(tc, f_atoms, f_bonds, adj, W_i_w, out):
                         )
                 dst = w_in[:, c, :].bitcast(F32).rearrange("p (h u) -> p h u", u=2)[:, 256 * half:256 * (half + 1), :]
                 src = wt[:].rearrange("p u h -> p h u")
-                if half == 0:
-                    nc.vector.tensor_copy(out=dst, in_=src)
-                else:
-                    nc.scalar.copy(out=dst, in_=src)
+                nc.scalar.copy(out=dst, in_=src)
         for c in range(2):
             nc.vector.quantize_mx(out=w_cd[:, c, :].bitcast(FP8X4), scales=w_sc[:, c, :], in_=w_in[:, c, :])
 
@@ -191,6 +195,5 @@ def tile_mpnencoder_pa_t_kernel(tc, f_atoms, f_bonds, adj, W_i_w, out):
                 gate1(g + 2)
             if g + 3 < NG:
                 flips(g + 3)
-            project(g)
-            if g + 3 < NG:
                 bonds(g + 3)
+            project(g)

@@ -31,7 +31,7 @@ def tile_mpnencoder_pa_t_kernel(tc, f_atoms, f_bonds, adj, W_i_w, out):
         keep = ctx.enter_context(tc.tile_pool(name="keep", bufs=1))
         st_in = ctx.enter_context(tc.tile_pool(name="st_in", bufs=4))
         st_cd = ctx.enter_context(tc.tile_pool(name="st_cd", bufs=3))
-        st_out = ctx.enter_context(tc.tile_pool(name="st_out", bufs=3))
+        st_out = ctx.enter_context(tc.tile_pool(name="st_out", bufs=6))
         ps_o = ctx.enter_context(tc.psum_pool(name="ps_o", bufs=4))
         ps_j = ctx.enter_context(tc.psum_pool(name="ps_j", bufs=2))
         ps_t = ctx.enter_context(tc.psum_pool(name="ps_t", bufs=2))
@@ -61,22 +61,13 @@ def tile_mpnencoder_pa_t_kernel(tc, f_atoms, f_bonds, adj, W_i_w, out):
         out_v = out.rearrange("b m n h -> (b m) n h")
 
         make_identity(nc, ident[:])
-        nc.vector.memset(b_sb[:, N * BB:N * BB + 192], 0.0)
+        nc.gpsimd.memset(b_sb[:, N * BB:N * BB + 192], 0.0)
         nc.vector.tensor_copy(out=adj2[:], in_=adj_sb[:].unsqueeze(2).to_broadcast([P, N, 2]))
 
         adj2_w = adj2[:].rearrange("p n e -> p (n e)").bitcast(F32)
         fa_w = fa_sb[:].bitcast(F32)
         b_w = b_sb[:].bitcast(F32)
         w_w = w_sb[:].bitcast(F32)
-
-        ft = ps_t.tile([P, 3, P], F32, tag="T", name="ft")
-        for k, first in enumerate((0, 128, 224)):
-            nc.tensor.transpose(ft[:, k, :], fa_w[:, first:first + P], ident[:])
-        nc.vector.tensor_copy(
-            out=fa_t0[:].bitcast(F32).rearrange("p (w u) -> p w u", u=2),
-            in_=ft[:, 0:2, :].rearrange("p u w -> p w u"),
-        )
-        nc.scalar.copy(out=f1[:], in_=ft[:, 2:3, :].to_broadcast([P, NS, P]))
 
         def twice(words, s):
             return (
@@ -91,17 +82,23 @@ def tile_mpnencoder_pa_t_kernel(tc, f_atoms, f_bonds, adj, W_i_w, out):
         in_of = {}
         cd_of = {}
 
-        def flips(g):
+        def spread(g):
             j_ps = ps_j.tile([P, G, P], F32, tag="J", name="j_ps")
-            t_ps = ps_t.tile([P, G, P], F32, tag="T", name="t_ps")
             for i in range(SIZES[g]):
                 n = FIRST[g] + i
                 nc.tensor.transpose(j_ps[:, i, :], adj2_w[:, n:n + 1].to_broadcast([P, P]), ident[:])
+            j_of[g] = j_ps
+
+        def flip_bonds(g):
+            t_ps = ps_t.tile([P, G, P], F32, tag="T", name="t_ps")
             for i in range(SIZES[g]):
                 n = FIRST[g] + i
                 nc.tensor.transpose(t_ps[:, i, :], b_w[:, 32 * n:32 * n + P], ident[:])
-            j_of[g] = j_ps
             t_of[g] = t_ps
+
+        def flips(g):
+            spread(g)
+            flip_bonds(g)
 
         def slot(g):
             return G * (g % 2)
@@ -158,18 +155,15 @@ def tile_mpnencoder_pa_t_kernel(tc, f_atoms, f_bonds, adj, W_i_w, out):
                         stop=(c == 1),
                     )
                 nc.scalar.copy(out=o_sb[:, i, :], in_=o_ps[:])
-            nc.sync.dma_start(out=out_v[:, FIRST[g]:FIRST[g] + s, :], in_=o_sb[:, 0:s, :])
+                if i % 2 == 1 or i == s - 1:
+                    lo = i - i % 2
+                    nc.sync.dma_start(out=out_v[:, FIRST[g] + lo:FIRST[g] + i + 1, :], in_=o_sb[:, lo:i + 1, :])
 
-        flips(0)
-        bonds(0)
-        flips(1)
-        bonds(1)
-        gate0(0)
-        gate1(0)
-        gate0(1)
-        gate1(1)
+        def gate(g):
+            gate0(g)
+            gate1(g)
 
-        for c in range(2):
+        def flip_w(c):
             for half in range(2):
                 wt = ps_o.tile([P, 2, 256], F32, tag="O", name="wt")
                 for u in range(2):
@@ -180,20 +174,44 @@ def tile_mpnencoder_pa_t_kernel(tc, f_atoms, f_bonds, adj, W_i_w, out):
                             ident[:],
                         )
                 dst = w_in[:, c, :].bitcast(F32).rearrange("p (h u) -> p h u", u=2)[:, 256 * half:256 * (half + 1), :]
-                src = wt[:].rearrange("p u h -> p h u")
-                nc.scalar.copy(out=dst, in_=src)
-        for c in range(2):
-            nc.vector.quantize_mx(out=w_cd[:, c, :].bitcast(FP8X4), scales=w_sc[:, c, :], in_=w_in[:, c, :])
+                nc.scalar.copy(out=dst, in_=wt[:].rearrange("p u h -> p h u"))
 
+        spread(0)
+        ft = ps_t.tile([P, 3, P], F32, tag="T", name="ft")
+        for k, first in enumerate((0, 128, 224)):
+            nc.tensor.transpose(ft[:, k, :], fa_w[:, first:first + P], ident[:])
+        nc.vector.tensor_copy(
+            out=fa_t0[:].bitcast(F32).rearrange("p (w u) -> p w u", u=2),
+            in_=ft[:, 0:2, :].rearrange("p u w -> p w u"),
+        )
+        nc.scalar.copy(out=f1[:], in_=ft[:, 2:3, :].to_broadcast([P, NS, P]))
+        flip_bonds(0)
+        bonds(0)
+        flips(1)
+        bonds(1)
+        gate(0)
+        gate(1)
+        flip_w(0)
         flips(2)
         bonds(2)
-        for g in range(NG):
-            if g + 2 < NG:
-                gate0(g + 2)
-            quant(g)
-            if g + 2 < NG:
-                gate1(g + 2)
-            if g + 3 < NG:
-                flips(g + 3)
-                bonds(g + 3)
-            project(g)
+        flip_w(1)
+        gate(2)
+        for c in range(2):
+            nc.vector.quantize_mx(out=w_cd[:, c, :].bitcast(FP8X4), scales=w_sc[:, c, :], in_=w_in[:, c, :])
+        flips(3)
+        bonds(3)
+        flips(4)
+        bonds(4)
+        quant(0)
+        project(0)
+        quant(1)
+        project(1)
+        for k in range(3, NG):
+            gate(k)
+            quant(k - 1)
+            if k + 2 < NG:
+                flips(k + 2)
+                bonds(k + 2)
+            project(k - 1)
+        quant(NG - 1)
+        project(NG - 1)

@@ -18,7 +18,6 @@ H = 512
 G = 4
 SIZES = (4,) * 15 + (2, 1, 1)
 NG = len(SIZES)
-NS = 2 * G
 FLOPS = 2 * 2 * N * N * 1024 * H
 
 W_BLOCKS = ((0, 0, 512), (512, 896, 64), (576, 512, 192), (768, 960, 64), (832, 704, 192))
@@ -29,12 +28,13 @@ def tile_mpnencoder_pa_t_kernel(tc, f_atoms, f_bonds, adj, W_i_w, out):
     FIRST = [sum(SIZES[:g]) for g in range(NG)]
     with ExitStack() as ctx:
         keep = ctx.enter_context(tc.tile_pool(name="keep", bufs=1))
-        st_in = ctx.enter_context(tc.tile_pool(name="st_in", bufs=4))
+        st_g = ctx.enter_context(tc.tile_pool(name="st_g", bufs=4))
+        st_in = ctx.enter_context(tc.tile_pool(name="st_in", bufs=5))
         st_cd = ctx.enter_context(tc.tile_pool(name="st_cd", bufs=3))
         st_out = ctx.enter_context(tc.tile_pool(name="st_out", bufs=6))
         ps_o = ctx.enter_context(tc.psum_pool(name="ps_o", bufs=4))
         ps_j = ctx.enter_context(tc.psum_pool(name="ps_j", bufs=2))
-        ps_t = ctx.enter_context(tc.psum_pool(name="ps_t", bufs=2))
+        ps_t = ctx.enter_context(tc.psum_pool(name="ps_t", bufs=1))
         ctx.enter_context(tc.manual_schedule())
 
         ident = keep.tile([P, P], F32, name="ident")
@@ -42,8 +42,8 @@ def tile_mpnencoder_pa_t_kernel(tc, f_atoms, f_bonds, adj, W_i_w, out):
         adj2 = keep.tile([P, N, 2], BF16, name="adj2")
         fa_sb = keep.tile([P, AB], BF16, name="fa_sb")
         fa_t0 = keep.tile([P, 512], BF16, name="fa_t0")
-        f1 = keep.tile([P, NS, P], F32, name="f1")
-        b_sb = keep.tile([P, N * BB + 192], BF16, name="b_sb")
+        adj_f = keep.tile([P, N], F32, name="adj_f")
+        b_sb = keep.tile([P, N * BB], BF16, name="b_sb")
         w_sb = keep.tile([P, 4, 1024], BF16, name="w_sb")
         w_in = keep.tile([P, 2, 2048], BF16, name="w_in", align_bytes=64)
         w_cd = keep.tile([P, 2, H], U32, name="w_cd", align_bytes=64)
@@ -61,12 +61,11 @@ def tile_mpnencoder_pa_t_kernel(tc, f_atoms, f_bonds, adj, W_i_w, out):
         out_v = out.rearrange("b m n h -> (b m) n h")
 
         make_identity(nc, ident[:])
-        nc.gpsimd.memset(b_sb[:, N * BB:N * BB + 192], 0.0)
+        nc.gpsimd.tensor_copy(out=adj_f[:], in_=adj_sb[:])
         nc.vector.tensor_copy(out=adj2[:], in_=adj_sb[:].unsqueeze(2).to_broadcast([P, N, 2]))
 
         adj2_w = adj2[:].rearrange("p n e -> p (n e)").bitcast(F32)
         fa_w = fa_sb[:].bitcast(F32)
-        b_w = b_sb[:].bitcast(F32)
         w_w = w_sb[:].bitcast(F32)
 
         def twice(words, s):
@@ -78,6 +77,7 @@ def tile_mpnencoder_pa_t_kernel(tc, f_atoms, f_bonds, adj, W_i_w, out):
             )
 
         j_of = {}
+        gn_of = {}
         t_of = {}
         in_of = {}
         cd_of = {}
@@ -89,40 +89,52 @@ def tile_mpnencoder_pa_t_kernel(tc, f_atoms, f_bonds, adj, W_i_w, out):
                 nc.tensor.transpose(j_ps[:, i, :], adj2_w[:, n:n + 1].to_broadcast([P, P]), ident[:])
             j_of[g] = j_ps
 
-        def flip_bonds(g):
-            t_ps = ps_t.tile([P, G, P], F32, tag="T", name="t_ps")
+        def natural(g):
+            gn = st_g.tile([P, G, 256], BF16, tag="GN", name="gn")
+            gn_of[g] = gn
             for i in range(SIZES[g]):
                 n = FIRST[g] + i
-                nc.tensor.transpose(t_ps[:, i, :], b_w[:, 32 * n:32 * n + P], ident[:])
-            t_of[g] = t_ps
+                for lo, hi, src in ((0, BB, b_sb[:, BB * n:BB * (n + 1)]), (BB, 256, fa_sb[:, 512:AB])):
+                    nc.gpsimd.tensor_scalar(
+                        out=gn[:, i, lo:hi],
+                        in0=src,
+                        scalar1=adj_f[:, n:n + 1],
+                        scalar2=0.0,
+                        op0=MULT,
+                        op1=mybir.AluOpType.add,
+                    )
 
-        def flips(g):
-            spread(g)
-            flip_bonds(g)
-
-        def slot(g):
-            return G * (g % 2)
-
-        def bonds(g):
+        def halves(g):
             s = SIZES[g]
-            nc.scalar.copy(out=f1[0:32, slot(g):slot(g) + s, :], in_=t_of[g][0:32, 0:s, :])
+            return ((0, (s + 1) // 2), ((s + 1) // 2, s))
+
+        def flip_natural(g):
+            for h, (lo, hi) in enumerate(halves(g)):
+                if lo == hi:
+                    continue
+                t_ps = ps_t.tile([P, G, P], F32, tag=("TS", "TV")[h], name="t_ps")
+                for i in range(lo, hi):
+                    nc.tensor.transpose(t_ps[:, i - lo, :], gn_of[g][:, i, :].bitcast(F32), ident[:])
+                t_of[g, h] = t_ps
+
+        def new_in(g):
+            in_of[g] = st_in.tile([P, G, 2, 512], BF16, tag="IN", name="g_in", align_bytes=64)
+
+        def copy_out(g, h):
+            lo, hi = halves(g)[h]
+            if lo == hi:
+                return
+            engine_copy = (nc.scalar.copy, nc.vector.tensor_copy)[h]
+            engine_copy(
+                out=in_of[g][:, lo:hi, 1, :].bitcast(F32).rearrange("p n (w u) -> p n w u", u=2),
+                in_=t_of[g, h][:, 0:hi - lo, :].unsqueeze(3).to_broadcast([P, hi - lo, P, 2]),
+            )
 
         def gate0(g):
             s = SIZES[g]
-            g_in = st_in.tile([P, G, 2, 512], BF16, tag="IN", name="g_in", align_bytes=64)
-            in_of[g] = g_in
             nc.vector.tensor_tensor(
-                out=g_in[:, 0:s, 0, :].rearrange("p n (w u e) -> p n w u e", u=2, e=2),
+                out=in_of[g][:, 0:s, 0, :].rearrange("p n (w u e) -> p n w u e", u=2, e=2),
                 in0=fa_t0[:].rearrange("p (w u e) -> p w u e", u=2, e=2).unsqueeze(1).to_broadcast([P, s, P, 2, 2]),
-                in1=twice(j_of[g][:, 0:s, :], s),
-                op=MULT,
-            )
-
-        def gate1(g):
-            s = SIZES[g]
-            nc.vector.tensor_tensor(
-                out=in_of[g][:, 0:s, 1, :].rearrange("p n (w u e) -> p n w u e", u=2, e=2),
-                in0=twice(f1[:, slot(g):slot(g) + s, :], s),
                 in1=twice(j_of[g][:, 0:s, :], s),
                 op=MULT,
             )
@@ -159,10 +171,6 @@ def tile_mpnencoder_pa_t_kernel(tc, f_atoms, f_bonds, adj, W_i_w, out):
                     lo = i - i % 2
                     nc.sync.dma_start(out=out_v[:, FIRST[g] + lo:FIRST[g] + i + 1, :], in_=o_sb[:, lo:i + 1, :])
 
-        def gate(g):
-            gate0(g)
-            gate1(g)
-
         def flip_w(c):
             for half in range(2):
                 wt = ps_o.tile([P, 2, 256], F32, tag="O", name="wt")
@@ -176,42 +184,56 @@ def tile_mpnencoder_pa_t_kernel(tc, f_atoms, f_bonds, adj, W_i_w, out):
                 dst = w_in[:, c, :].bitcast(F32).rearrange("p (h u) -> p h u", u=2)[:, 256 * half:256 * (half + 1), :]
                 nc.scalar.copy(out=dst, in_=wt[:].rearrange("p u h -> p h u"))
 
+        natural(0)
+        natural(1)
+        natural(2)
+        natural(3)
+        for g in range(3):
+            new_in(g)
         spread(0)
-        ft = ps_t.tile([P, 3, P], F32, tag="T", name="ft")
-        for k, first in enumerate((0, 128, 224)):
-            nc.tensor.transpose(ft[:, k, :], fa_w[:, first:first + P], ident[:])
+        ft = ps_o.tile([P, 2, P], F32, tag="O", name="ft")
+        for u in range(2):
+            nc.tensor.transpose(ft[:, u, :], fa_w[:, P * u:P * (u + 1)], ident[:])
         nc.vector.tensor_copy(
             out=fa_t0[:].bitcast(F32).rearrange("p (w u) -> p w u", u=2),
-            in_=ft[:, 0:2, :].rearrange("p u w -> p w u"),
+            in_=ft[:].rearrange("p u w -> p w u"),
         )
-        nc.scalar.copy(out=f1[:], in_=ft[:, 2:3, :].to_broadcast([P, NS, P]))
-        flip_bonds(0)
-        bonds(0)
-        flips(1)
-        bonds(1)
-        gate(0)
-        gate(1)
+        spread(1)
+        flip_natural(0)
+        copy_out(0, 0)
+        gate0(0)
+        copy_out(0, 1)
+        gate0(1)
         flip_w(0)
-        flips(2)
-        bonds(2)
         flip_w(1)
-        gate(2)
+        flip_natural(1)
+        copy_out(1, 0)
         for c in range(2):
             nc.vector.quantize_mx(out=w_cd[:, c, :].bitcast(FP8X4), scales=w_sc[:, c, :], in_=w_in[:, c, :])
-        flips(3)
-        bonds(3)
-        flips(4)
-        bonds(4)
         quant(0)
+        spread(2)
         project(0)
+        copy_out(1, 1)
         quant(1)
+        flip_natural(2)
+        copy_out(2, 0)
+        spread(3)
         project(1)
-        for k in range(3, NG):
-            gate(k)
-            quant(k - 1)
+        for k in range(2, NG):
             if k + 2 < NG:
-                flips(k + 2)
-                bonds(k + 2)
-            project(k - 1)
+                natural(k + 2)
+            if k + 1 < NG:
+                new_in(k + 1)
+            gate0(k)
+            copy_out(k, 1)
+            if k > 2:
+                quant(k - 1)
+            if k + 1 < NG:
+                flip_natural(k + 1)
+                copy_out(k + 1, 0)
+            if k + 2 < NG:
+                spread(k + 2)
+            if k > 2:
+                project(k - 1)
         quant(NG - 1)
         project(NG - 1)

@@ -42,7 +42,6 @@ def tile_mpnencoder_pa_t_kernel(tc, f_atoms, f_bonds, adj, W_i_w, out):
         adj2 = keep.tile([P, N, 2], BF16, name="adj2")
         fa_sb = keep.tile([P, AB], BF16, name="fa_sb")
         fa_t0 = keep.tile([P, 512], BF16, name="fa_t0")
-        adj_f = keep.tile([P, N], F32, name="adj_f")
         b_sb = keep.tile([P, N * BB], BF16, name="b_sb")
         w_sb = keep.tile([P, 4, 1024], BF16, name="w_sb")
         w_in = keep.tile([P, 2, 2048], BF16, name="w_in", align_bytes=64)
@@ -61,7 +60,6 @@ def tile_mpnencoder_pa_t_kernel(tc, f_atoms, f_bonds, adj, W_i_w, out):
         out_v = out.rearrange("b m n h -> (b m) n h")
 
         make_identity(nc, ident[:])
-        nc.gpsimd.tensor_copy(out=adj_f[:], in_=adj_sb[:])
         nc.vector.tensor_copy(out=adj2[:], in_=adj_sb[:].unsqueeze(2).to_broadcast([P, N, 2]))
 
         adj2_w = adj2[:].rearrange("p n e -> p (n e)").bitcast(F32)
@@ -92,21 +90,22 @@ def tile_mpnencoder_pa_t_kernel(tc, f_atoms, f_bonds, adj, W_i_w, out):
         def natural(g):
             gn = st_g.tile([P, G, 256], BF16, tag="GN", name="gn")
             gn_of[g] = gn
-            for i in range(SIZES[g]):
-                n = FIRST[g] + i
-                for lo, hi, src in ((0, BB, b_sb[:, BB * n:BB * (n + 1)]), (BB, 256, fa_sb[:, 512:AB])):
-                    nc.gpsimd.tensor_scalar(
-                        out=gn[:, i, lo:hi],
-                        in0=src,
-                        scalar1=adj_f[:, n:n + 1],
-                        scalar2=0.0,
-                        op0=MULT,
-                        op1=mybir.AluOpType.add,
-                    )
+            s, first = SIZES[g], FIRST[g]
+            nc.vector.tensor_tensor(
+                out=gn[:, 0:s, 0:BB].rearrange("p n (w e) -> p n w e", e=2),
+                in0=b_sb[:, BB * first:BB * (first + s)].rearrange("p (n w e) -> p n w e", w=BB // 2, e=2),
+                in1=adj2[:, first:first + s, :].unsqueeze(2).to_broadcast([P, s, BB // 2, 2]),
+                op=MULT,
+            )
+            for i in range(s):
+                nc.vector.tensor_scalar(
+                    out=gn[:, i, BB:256], in0=fa_sb[:, 512:AB], scalar1=adj_sb[:, first + i:first + i + 1], scalar2=None, op0=MULT
+                )
 
         def halves(g):
             s = SIZES[g]
-            return ((0, (s + 1) // 2), ((s + 1) // 2, s))
+            on_scalar = max(1, s - 1)
+            return ((0, on_scalar), (on_scalar, s))
 
         def flip_natural(g):
             for h, (lo, hi) in enumerate(halves(g)):
@@ -185,9 +184,6 @@ def tile_mpnencoder_pa_t_kernel(tc, f_atoms, f_bonds, adj, W_i_w, out):
                 nc.scalar.copy(out=dst, in_=wt[:].rearrange("p u h -> p h u"))
 
         natural(0)
-        natural(1)
-        natural(2)
-        natural(3)
         for g in range(3):
             new_in(g)
         spread(0)
@@ -202,6 +198,7 @@ def tile_mpnencoder_pa_t_kernel(tc, f_atoms, f_bonds, adj, W_i_w, out):
         flip_natural(0)
         copy_out(0, 0)
         gate0(0)
+        natural(1)
         copy_out(0, 1)
         gate0(1)
         flip_w(0)
@@ -214,17 +211,19 @@ def tile_mpnencoder_pa_t_kernel(tc, f_atoms, f_bonds, adj, W_i_w, out):
         spread(2)
         project(0)
         copy_out(1, 1)
+        natural(2)
         quant(1)
+        natural(3)
         flip_natural(2)
         copy_out(2, 0)
         spread(3)
         project(1)
         for k in range(2, NG):
-            if k + 2 < NG:
-                natural(k + 2)
             if k + 1 < NG:
                 new_in(k + 1)
             gate0(k)
+            if k + 2 < NG:
+                natural(k + 2)
             copy_out(k, 1)
             if k > 2:
                 quant(k - 1)

@@ -43,7 +43,7 @@ def tile_mpnencoder_pa_t_kernel(tc, f_atoms, f_bonds, adj, W_i_w, out):
         fa_sb = keep.tile([P, AB], BF16, name="fa_sb")
         fa_t0 = keep.tile([P, 512], BF16, name="fa_t0")
         b_sb = keep.tile([P, N * BB], BF16, name="b_sb")
-        w_sb = keep.tile([P, 4, 1024], BF16, name="w_sb")
+        w_sb = [keep.tile([P, 4, 512], BF16, name="w_sb0"), keep.tile([P, 4, 512], BF16, name="w_sb1")]
         w_in = keep.tile([P, 2, 2048], BF16, name="w_in", align_bytes=64)
         w_cd = keep.tile([P, 2, H], U32, name="w_cd", align_bytes=64)
         w_sc = keep.tile([P, 2, H], U8, name="w_sc", align_bytes=64)
@@ -54,7 +54,8 @@ def tile_mpnencoder_pa_t_kernel(tc, f_atoms, f_bonds, adj, W_i_w, out):
         nc.sync.dma_start(out=b_sb[:, 0:1024], in_=bonds_v[:, 0:1024])
         w_v = W_i_w.rearrange("(t p) f -> p t f", p=P)
         for dst, src, width in W_BLOCKS:
-            nc.sync.dma_start(out=w_sb[:, :, dst:dst + width], in_=w_v[:, :, src:src + width])
+            c, lo = divmod(dst, 512)
+            nc.sync.dma_start(out=w_sb[c][:, :, lo:lo + width], in_=w_v[:, :, src:src + width])
         for c in range(1, 4):
             nc.sync.dma_start(out=b_sb[:, 1024 * c:1024 * (c + 1)], in_=bonds_v[:, 1024 * c:1024 * (c + 1)])
         out_v = out.rearrange("b m n h -> (b m) n h")
@@ -64,7 +65,6 @@ def tile_mpnencoder_pa_t_kernel(tc, f_atoms, f_bonds, adj, W_i_w, out):
 
         adj2_w = adj2[:].rearrange("p n e -> p (n e)").bitcast(F32)
         fa_w = fa_sb[:].bitcast(F32)
-        w_w = w_sb[:].bitcast(F32)
 
         def twice(words, s):
             return (
@@ -104,7 +104,7 @@ def tile_mpnencoder_pa_t_kernel(tc, f_atoms, f_bonds, adj, W_i_w, out):
 
         def halves(g):
             s = SIZES[g]
-            on_scalar = max(1, s - 1)
+            on_scalar = s - 1
             return ((0, on_scalar), (on_scalar, s))
 
         def flip_natural(g):
@@ -117,7 +117,7 @@ def tile_mpnencoder_pa_t_kernel(tc, f_atoms, f_bonds, adj, W_i_w, out):
                 t_of[g, h] = t_ps
 
         def new_in(g):
-            in_of[g] = st_in.tile([P, G, 2, 512], BF16, tag="IN", name="g_in", align_bytes=64)
+            in_of[g] = st_in.tile([P, 2, SIZES[g], 512], BF16, tag="IN", name="g_in", align_bytes=64)
 
         def copy_out(g, h):
             lo, hi = halves(g)[h]
@@ -125,14 +125,14 @@ def tile_mpnencoder_pa_t_kernel(tc, f_atoms, f_bonds, adj, W_i_w, out):
                 return
             engine_copy = (nc.scalar.copy, nc.vector.tensor_copy)[h]
             engine_copy(
-                out=in_of[g][:, lo:hi, 1, :].bitcast(F32).rearrange("p n (w u) -> p n w u", u=2),
+                out=in_of[g][:, 1, lo:hi, :].bitcast(F32).rearrange("p n (w u) -> p n w u", u=2),
                 in_=t_of[g, h][:, 0:hi - lo, :].unsqueeze(3).to_broadcast([P, hi - lo, P, 2]),
             )
 
         def gate0(g):
             s = SIZES[g]
             nc.vector.tensor_tensor(
-                out=in_of[g][:, 0:s, 0, :].rearrange("p n (w u e) -> p n w u e", u=2, e=2),
+                out=in_of[g][:, 0].rearrange("p n (w u e) -> p n w u e", u=2, e=2),
                 in0=fa_t0[:].rearrange("p (w u e) -> p w u e", u=2, e=2).unsqueeze(1).to_broadcast([P, s, P, 2, 2]),
                 in1=twice(j_of[g][:, 0:s, :], s),
                 op=MULT,
@@ -140,35 +140,43 @@ def tile_mpnencoder_pa_t_kernel(tc, f_atoms, f_bonds, adj, W_i_w, out):
 
         def quant(g):
             s = SIZES[g]
-            cd = st_cd.tile([P, G, 2, P], U32, tag="CD", name="cd", align_bytes=64)
-            sc = st_cd.tile([P, G, 2, P], U8, tag="SC", name="sc", align_bytes=64)
+            cd = st_cd.tile([P, 2, s, P], U32, tag="CD", name="cd", align_bytes=64)
+            sc = st_cd.tile([P, 2, s, P], U8, tag="SC", name="sc", align_bytes=64)
             cd_of[g] = (cd, sc)
             nc.vector.quantize_mx(
-                out=cd[:, 0:s].rearrange("p n c w -> p (n c w)").bitcast(FP8X4),
-                scales=sc[:, 0:s].rearrange("p n c w -> p (n c w)"),
-                in_=in_of[g][:, 0:s].rearrange("p n c k -> p (n c k)"),
+                out=cd[:].rearrange("p c n w -> p (c n w)").bitcast(FP8X4),
+                scales=sc[:].rearrange("p c n w -> p (c n w)"),
+                in_=in_of[g][:].rearrange("p c n k -> p (c n k)"),
             )
 
-        def project(g):
+        o_of = {}
+
+        def multiply(g, i, c):
             cd, sc = cd_of[g]
+            if c == 0:
+                o_of[g, i] = ps_o.tile([P, H], F32, tag="O", name="o_ps")
+            nc.tensor.matmul_mx(
+                out=o_of[g, i][:],
+                lhsT=cd[:, c, i, :].bitcast(FP8X4),
+                lhsT_scale=sc[:, c, i, :],
+                rhs=w_cd[:, c, :].bitcast(FP8X4),
+                rhs_scale=w_sc[:, c, :],
+                start=(c == 0),
+                stop=(c == 1),
+            )
+
+        def drain(g, i, o_sb):
+            nc.scalar.copy(out=o_sb[:, i, :], in_=o_of[g, i][:])
+            if i % 2 == 1 or i == SIZES[g] - 1:
+                lo = i - i % 2
+                nc.sync.dma_start(out=out_v[:, FIRST[g] + lo:FIRST[g] + i + 1, :], in_=o_sb[:, lo:i + 1, :])
+
+        def project(g):
             o_sb = st_out.tile([P, G, H], F32, tag="OS", name="o_sb")
-            s = SIZES[g]
-            for i in range(s):
-                o_ps = ps_o.tile([P, H], F32, tag="O", name="o_ps")
+            for i in range(SIZES[g]):
                 for c in range(2):
-                    nc.tensor.matmul_mx(
-                        out=o_ps[:],
-                        lhsT=cd[:, i, c, :].bitcast(FP8X4),
-                        lhsT_scale=sc[:, i, c, :],
-                        rhs=w_cd[:, c, :].bitcast(FP8X4),
-                        rhs_scale=w_sc[:, c, :],
-                        start=(c == 0),
-                        stop=(c == 1),
-                    )
-                nc.scalar.copy(out=o_sb[:, i, :], in_=o_ps[:])
-                if i % 2 == 1 or i == s - 1:
-                    lo = i - i % 2
-                    nc.sync.dma_start(out=out_v[:, FIRST[g] + lo:FIRST[g] + i + 1, :], in_=o_sb[:, lo:i + 1, :])
+                    multiply(g, i, c)
+                drain(g, i, o_sb)
 
         def flip_w(c):
             for half in range(2):
@@ -177,15 +185,17 @@ def tile_mpnencoder_pa_t_kernel(tc, f_atoms, f_bonds, adj, W_i_w, out):
                     for t2 in range(2):
                         nc.tensor.transpose(
                             wt[:, u, P * t2:P * (t2 + 1)],
-                            w_w[:, 2 * half + t2, 256 * c + P * u:256 * c + P * (u + 1)],
+                            w_sb[c][:, 2 * half + t2, :].bitcast(F32)[:, P * u:P * (u + 1)],
                             ident[:],
                         )
                 dst = w_in[:, c, :].bitcast(F32).rearrange("p (h u) -> p h u", u=2)[:, 256 * half:256 * (half + 1), :]
                 nc.scalar.copy(out=dst, in_=wt[:].rearrange("p u h -> p h u"))
 
+        def quant_w(c):
+            nc.vector.quantize_mx(out=w_cd[:, c, :].bitcast(FP8X4), scales=w_sc[:, c, :], in_=w_in[:, c, :])
+
         natural(0)
-        for g in range(3):
-            new_in(g)
+        new_in(0)
         spread(0)
         ft = ps_o.tile([P, 2, P], F32, tag="O", name="ft")
         for u in range(2):
@@ -194,45 +204,40 @@ def tile_mpnencoder_pa_t_kernel(tc, f_atoms, f_bonds, adj, W_i_w, out):
             out=fa_t0[:].bitcast(F32).rearrange("p (w u) -> p w u", u=2),
             in_=ft[:].rearrange("p u w -> p w u"),
         )
-        spread(1)
         flip_natural(0)
         copy_out(0, 0)
         gate0(0)
-        natural(1)
+        spread(1)
         copy_out(0, 1)
-        gate0(1)
+        natural(1)
         flip_w(0)
-        flip_w(1)
-        flip_natural(1)
-        copy_out(1, 0)
-        for c in range(2):
-            nc.vector.quantize_mx(out=w_cd[:, c, :].bitcast(FP8X4), scales=w_sc[:, c, :], in_=w_in[:, c, :])
         quant(0)
+        flip_natural(1)
         spread(2)
-        project(0)
-        copy_out(1, 1)
+        flip_w(1)
+        quant_w(0)
         natural(2)
-        quant(1)
-        natural(3)
-        flip_natural(2)
-        copy_out(2, 0)
-        spread(3)
-        project(1)
-        for k in range(2, NG):
+        o_sb0 = st_out.tile([P, G, H], F32, tag="OS", name="o_sb")
+        for i in range(SIZES[0]):
+            multiply(0, i, 0)
+        quant_w(1)
+        for k in range(NG):
             if k + 1 < NG:
                 new_in(k + 1)
-            gate0(k)
-            if k + 2 < NG:
-                natural(k + 2)
-            copy_out(k, 1)
-            if k > 2:
-                quant(k - 1)
-            if k + 1 < NG:
-                flip_natural(k + 1)
                 copy_out(k + 1, 0)
+            if k == 0:
+                for i in range(SIZES[0]):
+                    multiply(0, i, 1)
+                    drain(0, i, o_sb0)
+            else:
+                project(k)
+            if k + 1 < NG:
+                gate0(k + 1)
+                copy_out(k + 1, 1)
+            if k + 3 < NG:
+                natural(k + 3)
+                spread(k + 3)
             if k + 2 < NG:
-                spread(k + 2)
-            if k > 2:
-                project(k - 1)
-        quant(NG - 1)
-        project(NG - 1)
+                flip_natural(k + 2)
+            if k + 1 < NG:
+                quant(k + 1)

@@ -16,8 +16,9 @@ AB = 704
 BB = 64
 H = 512
 G = 4
-SIZES = (4,) * 15 + (2, 1, 1)
-NG = len(SIZES)
+ON_S = 3
+NG = N // G
+PIECES = ((4,),) * (NG - 1) + ((2, 1, 1),)
 FLOPS = 2 * 2 * N * N * 1024 * H
 
 W_BLOCKS = ((0, 0, 512), (512, 896, 64), (576, 512, 192), (768, 960, 64), (832, 704, 192))
@@ -25,7 +26,6 @@ W_BLOCKS = ((0, 0, 512), (512, 896, 64), (576, 512, 192), (768, 960, 64), (832, 
 
 def tile_mpnencoder_pa_t_kernel(tc, f_atoms, f_bonds, adj, W_i_w, out):
     nc = tc.nc
-    FIRST = [sum(SIZES[:g]) for g in range(NG)]
     with ExitStack() as ctx:
         keep = ctx.enter_context(tc.tile_pool(name="keep", bufs=1))
         st_g = ctx.enter_context(tc.tile_pool(name="st_g", bufs=4))
@@ -51,13 +51,13 @@ def tile_mpnencoder_pa_t_kernel(tc, f_atoms, f_bonds, adj, W_i_w, out):
         nc.sync.dma_start(out=adj_sb[:], in_=adj.rearrange("b m n -> (b m) n"))
         nc.sync.dma_start(out=fa_sb[:], in_=f_atoms.rearrange("b m f -> (b m) f"))
         bonds_v = f_bonds.rearrange("b m n f -> (b m) (n f)")
-        nc.sync.dma_start(out=b_sb[:, 0:1024], in_=bonds_v[:, 0:1024])
+        nc.sync.dma_start(out=b_sb[:, 0:256], in_=bonds_v[:, 0:256])
         w_v = W_i_w.rearrange("(t p) f -> p t f", p=P)
         for dst, src, width in W_BLOCKS:
             c, lo = divmod(dst, 512)
             nc.sync.dma_start(out=w_sb[c][:, :, lo:lo + width], in_=w_v[:, :, src:src + width])
-        for c in range(1, 4):
-            nc.sync.dma_start(out=b_sb[:, 1024 * c:1024 * (c + 1)], in_=bonds_v[:, 1024 * c:1024 * (c + 1)])
+        for lo, hi in ((256, 1024), (1024, 2048), (2048, 3072), (3072, 4096)):
+            nc.sync.dma_start(out=b_sb[:, lo:hi], in_=bonds_v[:, lo:hi])
         out_v = out.rearrange("b m n h -> (b m) n h")
 
         make_identity(nc, ident[:])
@@ -79,84 +79,83 @@ def tile_mpnencoder_pa_t_kernel(tc, f_atoms, f_bonds, adj, W_i_w, out):
         t_of = {}
         in_of = {}
         cd_of = {}
+        o_of = {}
+
+        def start_of(g, q):
+            return G * g + sum(PIECES[g][:q])
 
         def spread(g):
             j_ps = ps_j.tile([P, G, P], F32, tag="J", name="j_ps")
-            for i in range(SIZES[g]):
-                n = FIRST[g] + i
+            for i in range(G):
+                n = G * g + i
                 nc.tensor.transpose(j_ps[:, i, :], adj2_w[:, n:n + 1].to_broadcast([P, P]), ident[:])
             j_of[g] = j_ps
 
         def natural(g):
             gn = st_g.tile([P, G, 256], BF16, tag="GN", name="gn")
             gn_of[g] = gn
-            s, first = SIZES[g], FIRST[g]
+            for i in range(G):
+                n = G * g + i
+                nc.vector.tensor_scalar(
+                    out=gn[:, i, BB:256], in0=fa_sb[:, 512:AB], scalar1=adj_sb[:, n:n + 1], scalar2=None, op0=MULT
+                )
             nc.vector.tensor_tensor(
-                out=gn[:, 0:s, 0:BB].rearrange("p n (w e) -> p n w e", e=2),
-                in0=b_sb[:, BB * first:BB * (first + s)].rearrange("p (n w e) -> p n w e", w=BB // 2, e=2),
-                in1=adj2[:, first:first + s, :].unsqueeze(2).to_broadcast([P, s, BB // 2, 2]),
+                out=gn[:, :, 0:BB].rearrange("p n (w e) -> p n w e", e=2),
+                in0=b_sb[:, BB * G * g:BB * G * (g + 1)].rearrange("p (n w e) -> p n w e", w=BB // 2, e=2),
+                in1=adj2[:, G * g:G * (g + 1), :].unsqueeze(2).to_broadcast([P, G, BB // 2, 2]),
                 op=MULT,
             )
-            for i in range(s):
-                nc.vector.tensor_scalar(
-                    out=gn[:, i, BB:256], in0=fa_sb[:, 512:AB], scalar1=adj_sb[:, first + i:first + i + 1], scalar2=None, op0=MULT
-                )
-
-        def halves(g):
-            s = SIZES[g]
-            on_scalar = s - 1
-            return ((0, on_scalar), (on_scalar, s))
 
         def flip_natural(g):
-            for h, (lo, hi) in enumerate(halves(g)):
-                if lo == hi:
-                    continue
+            for h, (lo, hi) in enumerate(((0, ON_S), (ON_S, G))):
                 t_ps = ps_t.tile([P, G, P], F32, tag=("TS", "TV")[h], name="t_ps")
                 for i in range(lo, hi):
                     nc.tensor.transpose(t_ps[:, i - lo, :], gn_of[g][:, i, :].bitcast(F32), ident[:])
                 t_of[g, h] = t_ps
 
         def new_in(g):
-            in_of[g] = st_in.tile([P, 2, SIZES[g], 512], BF16, tag="IN", name="g_in", align_bytes=64)
+            for q, s in enumerate(PIECES[g]):
+                in_of[g, q] = st_in.tile([P, 2, s, 512], BF16, tag="IN", name="g_in", align_bytes=64)
 
         def copy_out(g, h):
-            lo, hi = halves(g)[h]
-            if lo == hi:
-                return
             engine_copy = (nc.scalar.copy, nc.vector.tensor_copy)[h]
-            engine_copy(
-                out=in_of[g][:, 1, lo:hi, :].bitcast(F32).rearrange("p n (w u) -> p n w u", u=2),
-                in_=t_of[g, h][:, 0:hi - lo, :].unsqueeze(3).to_broadcast([P, hi - lo, P, 2]),
-            )
+            first, last = ((0, ON_S), (ON_S, G))[h]
+            for q, s in enumerate(PIECES[g]):
+                at = start_of(g, q) - G * g
+                lo, hi = max(first, at), min(last, at + s)
+                if lo < hi:
+                    engine_copy(
+                        out=in_of[g, q][:, 1, lo - at:hi - at, :].bitcast(F32).rearrange("p n (w u) -> p n w u", u=2),
+                        in_=t_of[g, h][:, lo - first:hi - first, :].unsqueeze(3).to_broadcast([P, hi - lo, P, 2]),
+                    )
 
-        def gate0(g):
-            s = SIZES[g]
+        def gate0(g, q=0):
+            s = PIECES[g][q]
+            at = start_of(g, q) - G * g
             nc.vector.tensor_tensor(
-                out=in_of[g][:, 0].rearrange("p n (w u e) -> p n w u e", u=2, e=2),
+                out=in_of[g, q][:, 0].rearrange("p n (w u e) -> p n w u e", u=2, e=2),
                 in0=fa_t0[:].rearrange("p (w u e) -> p w u e", u=2, e=2).unsqueeze(1).to_broadcast([P, s, P, 2, 2]),
-                in1=twice(j_of[g][:, 0:s, :], s),
+                in1=twice(j_of[g][:, at:at + s, :], s),
                 op=MULT,
             )
 
-        def quant(g):
-            s = SIZES[g]
+        def quant(g, q=0):
+            s = PIECES[g][q]
             cd = st_cd.tile([P, 2, s, P], U32, tag="CD", name="cd", align_bytes=64)
             sc = st_cd.tile([P, 2, s, P], U8, tag="SC", name="sc", align_bytes=64)
-            cd_of[g] = (cd, sc)
+            cd_of[g, q] = (cd, sc)
             nc.vector.quantize_mx(
                 out=cd[:].rearrange("p c n w -> p (c n w)").bitcast(FP8X4),
                 scales=sc[:].rearrange("p c n w -> p (c n w)"),
-                in_=in_of[g][:].rearrange("p c n k -> p (c n k)"),
+                in_=in_of[g, q][:].rearrange("p c n k -> p (c n k)"),
             )
 
-        o_of = {}
-
-        def multiply(g, i, c):
-            cd, sc = cd_of[g]
+        def multiply(g, q, i, c):
+            cd, sc = cd_of[g, q]
             if c == 0:
-                o_of[g, i] = ps_o.tile([P, H], F32, tag="O", name="o_ps")
+                o_of[g, q, i] = ps_o.tile([P, H], F32, tag="O", name="o_ps")
             nc.tensor.matmul_mx(
-                out=o_of[g, i][:],
+                out=o_of[g, q, i][:],
                 lhsT=cd[:, c, i, :].bitcast(FP8X4),
                 lhsT_scale=sc[:, c, i, :],
                 rhs=w_cd[:, c, :].bitcast(FP8X4),
@@ -165,18 +164,20 @@ def tile_mpnencoder_pa_t_kernel(tc, f_atoms, f_bonds, adj, W_i_w, out):
                 stop=(c == 1),
             )
 
-        def drain(g, i, o_sb):
-            nc.scalar.copy(out=o_sb[:, i, :], in_=o_of[g, i][:])
-            if i % 2 == 1 or i == SIZES[g] - 1:
+        def drain(g, q, i, o_sb):
+            nc.scalar.copy(out=o_sb[:, i, :], in_=o_of[g, q, i][:])
+            if i % 2 == 1 or i == PIECES[g][q] - 1:
                 lo = i - i % 2
-                nc.sync.dma_start(out=out_v[:, FIRST[g] + lo:FIRST[g] + i + 1, :], in_=o_sb[:, lo:i + 1, :])
+                n = start_of(g, q)
+                nc.sync.dma_start(out=out_v[:, n + lo:n + i + 1, :], in_=o_sb[:, lo:i + 1, :])
 
         def project(g):
-            o_sb = st_out.tile([P, G, H], F32, tag="OS", name="o_sb")
-            for i in range(SIZES[g]):
-                for c in range(2):
-                    multiply(g, i, c)
-                drain(g, i, o_sb)
+            for q, s in enumerate(PIECES[g]):
+                o_sb = st_out.tile([P, s, H], F32, tag="OS", name="o_sb")
+                for i in range(s):
+                    for c in range(2):
+                        multiply(g, q, i, c)
+                    drain(g, q, i, o_sb)
 
         def flip_w(c):
             for half in range(2):
@@ -196,14 +197,14 @@ def tile_mpnencoder_pa_t_kernel(tc, f_atoms, f_bonds, adj, W_i_w, out):
 
         natural(0)
         new_in(0)
-        spread(0)
         ft = ps_o.tile([P, 2, P], F32, tag="O", name="ft")
         for u in range(2):
             nc.tensor.transpose(ft[:, u, :], fa_w[:, P * u:P * (u + 1)], ident[:])
-        nc.vector.tensor_copy(
+        nc.scalar.copy(
             out=fa_t0[:].bitcast(F32).rearrange("p (w u) -> p w u", u=2),
             in_=ft[:].rearrange("p u w -> p w u"),
         )
+        spread(0)
         flip_natural(0)
         copy_out(0, 0)
         gate0(0)
@@ -212,32 +213,35 @@ def tile_mpnencoder_pa_t_kernel(tc, f_atoms, f_bonds, adj, W_i_w, out):
         natural(1)
         flip_w(0)
         quant(0)
+        flip_w(1)
         flip_natural(1)
         spread(2)
-        flip_w(1)
         quant_w(0)
-        natural(2)
         o_sb0 = st_out.tile([P, G, H], F32, tag="OS", name="o_sb")
-        for i in range(SIZES[0]):
-            multiply(0, i, 0)
+        for i in range(G):
+            multiply(0, 0, i, 0)
         quant_w(1)
         for k in range(NG):
             if k + 1 < NG:
                 new_in(k + 1)
                 copy_out(k + 1, 0)
             if k == 0:
-                for i in range(SIZES[0]):
-                    multiply(0, i, 1)
-                    drain(0, i, o_sb0)
+                for i in range(G):
+                    multiply(0, 0, i, 1)
+                    drain(0, 0, i, o_sb0)
             else:
                 project(k)
             if k + 1 < NG:
                 gate0(k + 1)
                 copy_out(k + 1, 1)
+            if k + 2 < NG:
+                natural(k + 2)
             if k + 3 < NG:
-                natural(k + 3)
                 spread(k + 3)
             if k + 2 < NG:
                 flip_natural(k + 2)
             if k + 1 < NG:
-                quant(k + 1)
+                for q in range(len(PIECES[k + 1])):
+                    if q > 0:
+                        gate0(k + 1, q)
+                    quant(k + 1, q)

@@ -16,8 +16,8 @@ AB = 704
 BB = 64
 H = 512
 G = 4
-ON_S = 3
 NG = N // G
+ON_S = (4, 4) + (3,) * (NG - 2)
 PIECES = ((4,),) * (NG - 1) + ((2, 1, 1),)
 FLOPS = 2 * 2 * N * N * 1024 * H
 
@@ -51,12 +51,12 @@ def tile_mpnencoder_pa_t_kernel(tc, f_atoms, f_bonds, adj, W_i_w, out):
         nc.sync.dma_start(out=adj_sb[:], in_=adj.rearrange("b m n -> (b m) n"))
         nc.sync.dma_start(out=fa_sb[:], in_=f_atoms.rearrange("b m f -> (b m) f"))
         bonds_v = f_bonds.rearrange("b m n f -> (b m) (n f)")
-        nc.sync.dma_start(out=b_sb[:, 0:256], in_=bonds_v[:, 0:256])
+        nc.sync.dma_start(out=b_sb[:, 0:512], in_=bonds_v[:, 0:512])
         w_v = W_i_w.rearrange("(t p) f -> p t f", p=P)
         for dst, src, width in W_BLOCKS:
             c, lo = divmod(dst, 512)
             nc.sync.dma_start(out=w_sb[c][:, :, lo:lo + width], in_=w_v[:, :, src:src + width])
-        for lo, hi in ((256, 1024), (1024, 2048), (2048, 3072), (3072, 4096)):
+        for lo, hi in ((512, 1024), (1024, 2048), (2048, 3072), (3072, 4096)):
             nc.sync.dma_start(out=b_sb[:, lo:hi], in_=bonds_v[:, lo:hi])
         out_v = out.rearrange("b m n h -> (b m) n h")
 
@@ -107,7 +107,9 @@ def tile_mpnencoder_pa_t_kernel(tc, f_atoms, f_bonds, adj, W_i_w, out):
             )
 
         def flip_natural(g):
-            for h, (lo, hi) in enumerate(((0, ON_S), (ON_S, G))):
+            for h, (lo, hi) in enumerate(((0, ON_S[g]), (ON_S[g], G))):
+                if lo == hi:
+                    continue
                 t_ps = ps_t.tile([P, G, P], F32, tag=("TS", "TV")[h], name="t_ps")
                 for i in range(lo, hi):
                     nc.tensor.transpose(t_ps[:, i - lo, :], gn_of[g][:, i, :].bitcast(F32), ident[:])
@@ -119,7 +121,7 @@ def tile_mpnencoder_pa_t_kernel(tc, f_atoms, f_bonds, adj, W_i_w, out):
 
         def copy_out(g, h):
             engine_copy = (nc.scalar.copy, nc.vector.tensor_copy)[h]
-            first, last = ((0, ON_S), (ON_S, G))[h]
+            first, last = ((0, ON_S[g]), (ON_S[g], G))[h]
             for q, s in enumerate(PIECES[g]):
                 at = start_of(g, q) - G * g
                 lo, hi = max(first, at), min(last, at + s)
@@ -165,14 +167,38 @@ def tile_mpnencoder_pa_t_kernel(tc, f_atoms, f_bonds, adj, W_i_w, out):
             )
 
         def drain(g, q, i, o_sb):
-            nc.scalar.copy(out=o_sb[:, i, :], in_=o_of[g, q, i][:])
-            if i % 2 == 1 or i == PIECES[g][q] - 1:
-                lo = i - i % 2
+            on_vector = g == NG - 1 and (start_of(g, q) + i) % 2 == 1
+            (nc.vector.tensor_copy if on_vector else nc.scalar.copy)(out=o_sb[:, i, :], in_=o_of[g, q, i][:])
+            if g >= NG - 2 or i % 2 == 1:
+                lo = i if g >= NG - 2 else i - 1
                 n = start_of(g, q)
                 nc.sync.dma_start(out=out_v[:, n + lo:n + i + 1, :], in_=o_sb[:, lo:i + 1, :])
 
+        def project_last():
+            q = len(PIECES[NG - 1]) - 1
+            cd, sc = cd_of[NG - 1, q]
+            for half in range(2):
+                cols = slice(H // 2 * half, H // 2 * (half + 1))
+                o_ps = ps_o.tile([P, H // 2], F32, tag="O", name="o_ps")
+                o_sb = st_out.tile([P, H // 2], F32, tag="OS", name="o_sb")
+                for c in range(2):
+                    nc.tensor.matmul_mx(
+                        out=o_ps[:],
+                        lhsT=cd[:, c, 0, :].bitcast(FP8X4),
+                        lhsT_scale=sc[:, c, 0, :],
+                        rhs=w_cd[:, c, cols].bitcast(FP8X4),
+                        rhs_scale=w_sc[:, c, cols],
+                        start=(c == 0),
+                        stop=(c == 1),
+                    )
+                (nc.scalar.copy, nc.vector.tensor_copy)[half](out=o_sb[:], in_=o_ps[:])
+                nc.sync.dma_start(out=out_v[:, N - 1, cols], in_=o_sb[:])
+
         def project(g):
             for q, s in enumerate(PIECES[g]):
+                if start_of(g, q) == N - 1:
+                    project_last()
+                    return
                 o_sb = st_out.tile([P, s, H], F32, tag="OS", name="o_sb")
                 for i in range(s):
                     for c in range(2):
@@ -197,6 +223,7 @@ def tile_mpnencoder_pa_t_kernel(tc, f_atoms, f_bonds, adj, W_i_w, out):
 
         natural(0)
         new_in(0)
+        new_in(1)
         ft = ps_o.tile([P, 2, P], F32, tag="O", name="ft")
         for u in range(2):
             nc.tensor.transpose(ft[:, u, :], fa_w[:, P * u:P * (u + 1)], ident[:])
@@ -220,10 +247,12 @@ def tile_mpnencoder_pa_t_kernel(tc, f_atoms, f_bonds, adj, W_i_w, out):
         o_sb0 = st_out.tile([P, G, H], F32, tag="OS", name="o_sb")
         for i in range(G):
             multiply(0, 0, i, 0)
+        gate0(1)
         quant_w(1)
         for k in range(NG):
             if k + 1 < NG:
-                new_in(k + 1)
+                if k > 0:
+                    new_in(k + 1)
                 copy_out(k + 1, 0)
             if k == 0:
                 for i in range(G):
@@ -232,7 +261,8 @@ def tile_mpnencoder_pa_t_kernel(tc, f_atoms, f_bonds, adj, W_i_w, out):
             else:
                 project(k)
             if k + 1 < NG:
-                gate0(k + 1)
+                if k > 0:
+                    gate0(k + 1)
                 copy_out(k + 1, 1)
             if k + 2 < NG:
                 natural(k + 2)

from contextlib import ExitStack

import concourse.mybir as mybir
from concourse.masks import make_identity

F32 = mybir.dt.float32
BF16 = mybir.dt.bfloat16
U32 = mybir.dt.uint32
U8 = mybir.dt.uint8
FP8X4 = mybir.dt.float8_e4m3fn_x4
MULT = mybir.AluOpType.mult

P = 128
N = 64
AB = 704
BB = 64
H = 512
G = 4
NG = N // G
ON_S = (4, 4) + (3,) * (NG - 2)
PIECES = ((4,),) * (NG - 1) + ((2, 1, 1),)
FLOPS = 2 * 2 * N * N * 1024 * H

W_BLOCKS = ((0, 0, 512), (512, 896, 64), (576, 512, 192), (768, 960, 64), (832, 704, 192))


def tile_mpnencoder_pa_t_kernel(tc, f_atoms, f_bonds, adj, W_i_w, out):
    nc = tc.nc
    with ExitStack() as ctx:
        keep = ctx.enter_context(tc.tile_pool(name="keep", bufs=1))
        st_g = ctx.enter_context(tc.tile_pool(name="st_g", bufs=4))
        st_in = ctx.enter_context(tc.tile_pool(name="st_in", bufs=5))
        st_cd = ctx.enter_context(tc.tile_pool(name="st_cd", bufs=3))
        st_out = ctx.enter_context(tc.tile_pool(name="st_out", bufs=6))
        ps_o = ctx.enter_context(tc.psum_pool(name="ps_o", bufs=4))
        ps_j = ctx.enter_context(tc.psum_pool(name="ps_j", bufs=2))
        ps_t = ctx.enter_context(tc.psum_pool(name="ps_t", bufs=1))
        ctx.enter_context(tc.manual_schedule())

        ident = keep.tile([P, P], F32, name="ident")
        adj_sb = keep.tile([P, N], BF16, name="adj_sb")
        adj2 = keep.tile([P, N, 2], BF16, name="adj2")
        fa_sb = keep.tile([P, AB], BF16, name="fa_sb")
        fa_t0 = keep.tile([P, 512], BF16, name="fa_t0")
        b_sb = keep.tile([P, N * BB], BF16, name="b_sb")
        w_sb = [keep.tile([P, 4, 512], BF16, name="w_sb0"), keep.tile([P, 4, 512], BF16, name="w_sb1")]
        w_in = keep.tile([P, 2, 2048], BF16, name="w_in", align_bytes=64)
        w_cd = keep.tile([P, 2, H], U32, name="w_cd", align_bytes=64)
        w_sc = keep.tile([P, 2, H], U8, name="w_sc", align_bytes=64)

        nc.sync.dma_start(out=adj_sb[:], in_=adj.rearrange("b m n -> (b m) n"))
        nc.sync.dma_start(out=fa_sb[:], in_=f_atoms.rearrange("b m f -> (b m) f"))
        bonds_v = f_bonds.rearrange("b m n f -> (b m) (n f)")
        nc.sync.dma_start(out=b_sb[:, 0:512], in_=bonds_v[:, 0:512])
        w_v = W_i_w.rearrange("(t p) f -> p t f", p=P)
        for dst, src, width in W_BLOCKS:
            c, lo = divmod(dst, 512)
            nc.sync.dma_start(out=w_sb[c][:, :, lo:lo + width], in_=w_v[:, :, src:src + width])
        for lo, hi in ((512, 1024), (1024, 2048), (2048, 3072), (3072, 4096)):
            nc.sync.dma_start(out=b_sb[:, lo:hi], in_=bonds_v[:, lo:hi])
        out_v = out.rearrange("b m n h -> (b m) n h")

        make_identity(nc, ident[:])
        nc.vector.tensor_copy(out=adj2[:], in_=adj_sb[:].unsqueeze(2).to_broadcast([P, N, 2]))

        adj2_w = adj2[:].rearrange("p n e -> p (n e)").bitcast(F32)
        fa_w = fa_sb[:].bitcast(F32)

        def twice(words, s):
            return (
                words.bitcast(BF16)
                .rearrange("p n (w e) -> p n w e", e=2)
                .unsqueeze(3)
                .to_broadcast([P, s, P, 2, 2])
            )

        j_of = {}
        gn_of = {}
        t_of = {}
        in_of = {}
        cd_of = {}
        o_of = {}

        def start_of(g, q):
            return G * g + sum(PIECES[g][:q])

        def spread(g):
            j_ps = ps_j.tile([P, G, P], F32, tag="J", name="j_ps")
            for i in range(G):
                n = G * g + i
                nc.tensor.transpose(j_ps[:, i, :], adj2_w[:, n:n + 1].to_broadcast([P, P]), ident[:])
            j_of[g] = j_ps

        def natural(g):
            gn = st_g.tile([P, G, 256], BF16, tag="GN", name="gn")
            gn_of[g] = gn
            for i in range(G):
                n = G * g + i
                nc.vector.tensor_scalar(
                    out=gn[:, i, BB:256], in0=fa_sb[:, 512:AB], scalar1=adj_sb[:, n:n + 1], scalar2=None, op0=MULT
                )
            nc.vector.tensor_tensor(
                out=gn[:, :, 0:BB].rearrange("p n (w e) -> p n w e", e=2),
                in0=b_sb[:, BB * G * g:BB * G * (g + 1)].rearrange("p (n w e) -> p n w e", w=BB // 2, e=2),
                in1=adj2[:, G * g:G * (g + 1), :].unsqueeze(2).to_broadcast([P, G, BB // 2, 2]),
                op=MULT,
            )

        def flip_natural(g):
            for h, (lo, hi) in enumerate(((0, ON_S[g]), (ON_S[g], G))):
                if lo == hi:
                    continue
                t_ps = ps_t.tile([P, G, P], F32, tag=("TS", "TV")[h], name="t_ps")
                for i in range(lo, hi):
                    nc.tensor.transpose(t_ps[:, i - lo, :], gn_of[g][:, i, :].bitcast(F32), ident[:])
                t_of[g, h] = t_ps

        def new_in(g):
            for q, s in enumerate(PIECES[g]):
                in_of[g, q] = st_in.tile([P, 2, s, 512], BF16, tag="IN", name="g_in", align_bytes=64)

        def copy_out(g, h):
            engine_copy = (nc.scalar.copy, nc.vector.tensor_copy)[h]
            first, last = ((0, ON_S[g]), (ON_S[g], G))[h]
            for q, s in enumerate(PIECES[g]):
                at = start_of(g, q) - G * g
                lo, hi = max(first, at), min(last, at + s)
                if lo < hi:
                    engine_copy(
                        out=in_of[g, q][:, 1, lo - at:hi - at, :].bitcast(F32).rearrange("p n (w u) -> p n w u", u=2),
                        in_=t_of[g, h][:, lo - first:hi - first, :].unsqueeze(3).to_broadcast([P, hi - lo, P, 2]),
                    )

        def gate0(g, q=0):
            s = PIECES[g][q]
            at = start_of(g, q) - G * g
            nc.vector.tensor_tensor(
                out=in_of[g, q][:, 0].rearrange("p n (w u e) -> p n w u e", u=2, e=2),
                in0=fa_t0[:].rearrange("p (w u e) -> p w u e", u=2, e=2).unsqueeze(1).to_broadcast([P, s, P, 2, 2]),
                in1=twice(j_of[g][:, at:at + s, :], s),
                op=MULT,
            )

        def quant(g, q=0):
            s = PIECES[g][q]
            cd = st_cd.tile([P, 2, s, P], U32, tag="CD", name="cd", align_bytes=64)
            sc = st_cd.tile([P, 2, s, P], U8, tag="SC", name="sc", align_bytes=64)
            cd_of[g, q] = (cd, sc)
            nc.vector.quantize_mx(
                out=cd[:].rearrange("p c n w -> p (c n w)").bitcast(FP8X4),
                scales=sc[:].rearrange("p c n w -> p (c n w)"),
                in_=in_of[g, q][:].rearrange("p c n k -> p (c n k)"),
            )

        def multiply(g, q, i, c):
            cd, sc = cd_of[g, q]
            if c == 0:
                o_of[g, q, i] = ps_o.tile([P, H], F32, tag="O", name="o_ps")
            nc.tensor.matmul_mx(
                out=o_of[g, q, i][:],
                lhsT=cd[:, c, i, :].bitcast(FP8X4),
                lhsT_scale=sc[:, c, i, :],
                rhs=w_cd[:, c, :].bitcast(FP8X4),
                rhs_scale=w_sc[:, c, :],
                start=(c == 0),
                stop=(c == 1),
            )

        def drain(g, q, i, o_sb):
            on_vector = g == NG - 1 and (start_of(g, q) + i) % 2 == 1
            (nc.vector.tensor_copy if on_vector else nc.scalar.copy)(out=o_sb[:, i, :], in_=o_of[g, q, i][:])
            if g >= NG - 2 or i % 2 == 1:
                lo = i if g >= NG - 2 else i - 1
                n = start_of(g, q)
                nc.sync.dma_start(out=out_v[:, n + lo:n + i + 1, :], in_=o_sb[:, lo:i + 1, :])

        def project_last():
            q = len(PIECES[NG - 1]) - 1
            cd, sc = cd_of[NG - 1, q]
            for half in range(2):
                cols = slice(H // 2 * half, H // 2 * (half + 1))
                o_ps = ps_o.tile([P, H // 2], F32, tag="O", name="o_ps")
                o_sb = st_out.tile([P, H // 2], F32, tag="OS", name="o_sb")
                for c in range(2):
                    nc.tensor.matmul_mx(
                        out=o_ps[:],
                        lhsT=cd[:, c, 0, :].bitcast(FP8X4),
                        lhsT_scale=sc[:, c, 0, :],
                        rhs=w_cd[:, c, cols].bitcast(FP8X4),
                        rhs_scale=w_sc[:, c, cols],
                        start=(c == 0),
                        stop=(c == 1),
                    )
                (nc.scalar.copy, nc.vector.tensor_copy)[half](out=o_sb[:], in_=o_ps[:])
                nc.sync.dma_start(out=out_v[:, N - 1, cols], in_=o_sb[:])

        def project(g):
            for q, s in enumerate(PIECES[g]):
                if start_of(g, q) == N - 1:
                    project_last()
                    return
                o_sb = st_out.tile([P, s, H], F32, tag="OS", name="o_sb")
                for i in range(s):
                    for c in range(2):
                        multiply(g, q, i, c)
                    drain(g, q, i, o_sb)

        def flip_w(c):
            for half in range(2):
                wt = ps_o.tile([P, 2, 256], F32, tag="O", name="wt")
                for u in range(2):
                    for t2 in range(2):
                        nc.tensor.transpose(
                            wt[:, u, P * t2:P * (t2 + 1)],
                            w_sb[c][:, 2 * half + t2, :].bitcast(F32)[:, P * u:P * (u + 1)],
                            ident[:],
                        )
                dst = w_in[:, c, :].bitcast(F32).rearrange("p (h u) -> p h u", u=2)[:, 256 * half:256 * (half + 1), :]
                nc.scalar.copy(out=dst, in_=wt[:].rearrange("p u h -> p h u"))

        def quant_w(c):
            nc.vector.quantize_mx(out=w_cd[:, c, :].bitcast(FP8X4), scales=w_sc[:, c, :], in_=w_in[:, c, :])

        natural(0)
        new_in(0)
        new_in(1)
        ft = ps_o.tile([P, 2, P], F32, tag="O", name="ft")
        for u in range(2):
            nc.tensor.transpose(ft[:, u, :], fa_w[:, P * u:P * (u + 1)], ident[:])
        nc.scalar.copy(
            out=fa_t0[:].bitcast(F32).rearrange("p (w u) -> p w u", u=2),
            in_=ft[:].rearrange("p u w -> p w u"),
        )
        spread(0)
        flip_natural(0)
        copy_out(0, 0)
        gate0(0)
        spread(1)
        copy_out(0, 1)
        natural(1)
        flip_w(0)
        quant(0)
        flip_w(1)
        flip_natural(1)
        spread(2)
        quant_w(0)
        o_sb0 = st_out.tile([P, G, H], F32, tag="OS", name="o_sb")
        for i in range(G):
            multiply(0, 0, i, 0)
        gate0(1)
        quant_w(1)
        for k in range(NG):
            if k + 1 < NG:
                if k > 0:
                    new_in(k + 1)
                copy_out(k + 1, 0)
            if k == 0:
                for i in range(G):
                    multiply(0, 0, i, 1)
                    drain(0, 0, i, o_sb0)
            else:
                project(k)
            if k + 1 < NG:
                if k > 0:
                    gate0(k + 1)
                copy_out(k + 1, 1)
            if k + 2 < NG:
                natural(k + 2)
            if k + 3 < NG:
                spread(k + 3)
            if k + 2 < NG:
                flip_natural(k + 2)
            if k + 1 < NG:
                for q in range(len(PIECES[k + 1])):
                    if q > 0:
                        gate0(k + 1, q)
                    quant(k + 1, q)
